import numpy as np
import ml_dtypes


def mxq(x, axis, fmt="e4m3"):
    dtype, down = {"e4m3": (ml_dtypes.float8_e4m3fn, 7), "e5m2": (ml_dtypes.float8_e5m2, 14)}[fmt]
    v = np.moveaxis(np.asarray(x, np.float32).astype(ml_dtypes.bfloat16).astype(np.float64), axis, -1)
    blocks = v.reshape(v.shape[:-1] + (-1, 32))
    amax = np.abs(blocks).max(-1, keepdims=True)
    byte = np.maximum(np.where(amax > 0, np.frexp(amax)[1] - 1 + 127, 0) - down, 1)
    scale = np.exp2(byte - 127.0)
    codes = (blocks / scale).astype(np.float32).astype(dtype).astype(np.float64)
    return np.moveaxis((codes * scale).reshape(v.shape), -1, axis)


WIDE = False


def mx_kscale(k):
    if not WIDE:
        return np.ones(k)
    levels = np.array([20, -20, 10, -10, 0])
    a = np.random.permutation(np.resize(levels, k // 512 * 4)).reshape(k // 512, 4)
    idx = np.arange(k)
    return np.exp2(a[idx // 512, idx % 128 // 32])


BF16 = ml_dtypes.bfloat16


def bf(x):
    return np.asarray(x, np.float32).astype(BF16)


def f64(x):
    return np.asarray(x).astype(np.float64)


B, S, K, N = 4, 256, 4096, 1024
T = B * S

GRID_VALUES = np.array([-6.0, -4.0, -3.0, -2.0, -1.5, -1.0, -0.5, 0.0, 0.5, 1.0, 1.5, 2.0, 3.0, 4.0, 6.0], dtype=np.float32)


def setup_inputs():
    s = mx_kscale(T).reshape(B, S, 1)
    x = np.random.standard_normal((B, S, K)) * s
    weight = np.random.standard_normal((N, K)) * 0.02
    bias = np.random.standard_normal(N) * 0.3
    g = np.random.standard_normal((B, S, N)) * np.exp2(np.random.randint(-12, 1, (B, S, 1))) / s
    return {"x": bf(x), "weight": bf(weight), "bias": bf(bias), "grid": bf(GRID_VALUES), "grad_out": bf(g)}


def reference(x, weight, bias, grid, grad_out):
    x2d = f64(x).reshape(-1, x.shape[-1])
    g2d = f64(grad_out).reshape(-1, grad_out.shape[-1])
    return mxq(g2d, 0, "e5m2").T @ mxq(x2d, 0, "e4m3")

@@ -1,0 +1,163 @@
+from contextlib import ExitStack
+
+import concourse.mybir as mybir
+
+F32 = mybir.dt.float32
+BF16 = mybir.dt.bfloat16
+U32 = mybir.dt.uint32
+U8 = mybir.dt.uint8
+E4M3X4 = mybir.dt.float8_e4m3fn_x4
+E5M2X4 = mybir.dt.float8_e5m2_x4
+
+P = 128
+PACK = 4
+K_PASS = P * PACK
+TOKENS = 1024
+PASSES = TOKENS // K_PASS
+OUT_ROWS = 1024
+OUT_COLS = 4096
+M_TILE = 128
+N_TILE = 512
+M_TILES = OUT_ROWS // M_TILE
+N_TILES = OUT_COLS // N_TILE
+
+FLOPS = 2 * TOKENS * OUT_ROWS * OUT_COLS
+
+X_CHUNKS = (1024, 1024, 2048)
+STORE_TILES = 2
+VECTOR_EVAC = (3,)
+
+
+def tile_ant_linear_kernel(tc, x, weight, bias, grid, grad_out, out):
+    nc = tc.nc
+    x2 = x.flatten_outer_dims()
+    g2 = grad_out.flatten_outer_dims()
+
+    with ExitStack() as ctx:
+        raw = ctx.enter_context(tc.tile_pool(name="raw", bufs=1))
+        grp = ctx.enter_context(tc.tile_pool(name="grp", bufs=4))
+        keep = ctx.enter_context(tc.tile_pool(name="keep", bufs=1))
+        stage = ctx.enter_context(tc.tile_pool(name="stage", bufs=16))
+        psum = ctx.enter_context(tc.psum_pool(name="psum", bufs=8))
+
+        def load(src, c, col0, width, name):
+            t = raw.tile([P, PACK, width], BF16, name=name)
+            nc.sync.dma_start(
+                out=t[:],
+                in_=src[c * K_PASS : (c + 1) * K_PASS, col0 : col0 + width].rearrange(
+                    "(p j) w -> p j w", j=PACK
+                ),
+            )
+            return t
+
+        g_raw = [None, None]
+        x_raw = {}
+        starts = [sum(X_CHUNKS[:i]) for i in range(len(X_CHUNKS))]
+
+        def load_x(i, c):
+            t = load(x2, c, starts[i], X_CHUNKS[i], "xr%d_%d" % (i, c))
+            for n in range(starts[i] // N_TILE, (starts[i] + X_CHUNKS[i]) // N_TILE):
+                x_raw[(n, c)] = (t, n * N_TILE - starts[i])
+
+        g_raw[0] = load(g2, 0, 0, OUT_ROWS, "gr0")
+        load_x(0, 0)
+        g_raw[1] = load(g2, 1, 0, OUT_ROWS, "gr1")
+        load_x(0, 1)
+        for i in range(1, len(X_CHUNKS)):
+            for c in range(PASSES):
+                load_x(i, c)
+
+        g_codes = [keep.tile([P, OUT_ROWS], U32, name="gc%d" % c, align_bytes=64) for c in range(PASSES)]
+        g_scales = [keep.tile([P, OUT_ROWS], U8, name="gs%d" % c, align_bytes=64) for c in range(PASSES)]
+        x_codes = {}
+        x_scales = {}
+        for n in range(N_TILES):
+            for c in range(PASSES):
+                x_codes[(n, c)] = keep.tile([P, N_TILE], U32, name="xc%d_%d" % (n, c), align_bytes=64)
+                x_scales[(n, c)] = keep.tile([P, N_TILE], U8, name="xs%d_%d" % (n, c), align_bytes=64)
+
+        pending = []
+
+        def flush(keep_last):
+            while len(pending) > keep_last:
+                grouped, codes, scales, fmt = pending.pop(0)
+                nc.vector.quantize_mx(
+                    out=codes.bitcast(fmt),
+                    scales=scales,
+                    in_=grouped[:].rearrange("p w j -> p (w j)"),
+                )
+
+        def unit(src_tile, col0, codes, scales, fmt):
+            grouped = grp.tile([P, N_TILE, PACK], BF16, name="grouped", align_bytes=64)
+            nc.vector.tensor_copy(
+                out=grouped[:].rearrange("p (c i) t -> p c t i", i=4),
+                in_=src_tile[:, :, col0 : col0 + N_TILE].rearrange("p t (c i) -> p c t i", i=4),
+            )
+            pending.append((grouped, codes, scales, fmt))
+            flush(1)
+
+        def quantise_g(c):
+            for h in range(OUT_ROWS // N_TILE):
+                cols = slice(h * N_TILE, (h + 1) * N_TILE)
+                unit(g_raw[c], h * N_TILE, g_codes[c][:, cols], g_scales[c][:, cols], E5M2X4)
+
+        def quantise_x(n, c):
+            t, col0 = x_raw[(n, c)]
+            unit(t, col0, x_codes[(n, c)][:], x_scales[(n, c)][:], E4M3X4)
+
+        def mx(acc, n, m, c):
+            rows = slice(m * M_TILE, (m + 1) * M_TILE)
+            nc.tensor.matmul_mx(
+                out=acc[:],
+                lhsT=g_codes[c][:, rows].bitcast(E5M2X4),
+                lhsT_scale=g_scales[c][:, rows],
+                rhs=x_codes[(n, c)][:].bitcast(E4M3X4),
+                rhs_scale=x_scales[(n, c)][:],
+                start=(c == 0),
+                stop=(c == PASSES - 1),
+            )
+
+        stages = {}
+
+        def leave(acc, n, m):
+            group, part = divmod(n, STORE_TILES)
+            if part == 0:
+                stages[m] = stage.tile([P, STORE_TILES * N_TILE], F32, name="res")
+            res = stages[m]
+            dst = res[:, part * N_TILE : (part + 1) * N_TILE]
+            if m in VECTOR_EVAC:
+                nc.vector.tensor_copy(out=dst, in_=acc[:])
+            else:
+                nc.scalar.copy(out=dst, in_=acc[:])
+            if part == STORE_TILES - 1:
+                col0 = group * STORE_TILES * N_TILE
+                nc.sync.dma_start(
+                    out=out[m * M_TILE : (m + 1) * M_TILE, col0 : col0 + STORE_TILES * N_TILE],
+                    in_=res[:],
+                )
+
+        quantise_g(0)
+        quantise_x(0, 0)
+        quantise_g(1)
+        quantise_x(0, 1)
+        quantise_x(1, 0)
+        quantise_x(1, 1)
+        flush(0)
+
+        accs = [psum.tile([P, N_TILE], F32, name="acc") for m in range(M_TILES)]
+        for m in range(M_TILES):
+            mx(accs[m], 0, m, 0)
+        for m in range(M_TILES):
+            mx(accs[m], 0, m, 1)
+            leave(accs[m], 0, m)
+
+        for n in range(1, N_TILES):
+            if n + 1 < N_TILES:
+                quantise_x(n + 1, 0)
+                quantise_x(n + 1, 1)
+                flush(0)
+            for m in range(M_TILES):
+                acc = psum.tile([P, N_TILE], F32, name="acc")
+                mx(acc, n, m, 0)
+                mx(acc, n, m, 1)
+                leave(acc, n, m)

@@ -23,7 +23,7 @@ N_TILES = OUT_COLS // N_TILE
 
 FLOPS = 2 * TOKENS * OUT_ROWS * OUT_COLS
 
-X_CHUNKS = (1024, 1024, 2048)
+X_CHUNKS = (2048, 2048)
 STORE_TILES = 2
 VECTOR_EVAC = (3,)
 

@@ -23,9 +23,13 @@ N_TILES = OUT_COLS // N_TILE
 
 FLOPS = 2 * TOKENS * OUT_ROWS * OUT_COLS
 
-X_CHUNKS = (2048, 2048)
-STORE_TILES = 2
-VECTOR_EVAC = (3,)
+X_CHUNKS = (1024, 1024, 2048)
+STORE_GROUPS = ((0, 3, 0), (3, 3, 0), (6, 2, 0))
+PINNED = False
+
+
+def vector_empties(n, m):
+    return n >= 6 and m % 2 == 1
 
 
 def tile_ant_linear_kernel(tc, x, weight, bias, grid, grad_out, out):
@@ -34,14 +38,19 @@ def tile_ant_linear_kernel(tc, x, weight, bias, grid, grad_out, out):
     g2 = grad_out.flatten_outer_dims()
 
     with ExitStack() as ctx:
+        if PINNED:
+            ctx.enter_context(tc.manual_schedule())
+        slots = ctx.enter_context(tc.tile_pool(name="slots", bufs=15))
         raw = ctx.enter_context(tc.tile_pool(name="raw", bufs=1))
-        grp = ctx.enter_context(tc.tile_pool(name="grp", bufs=4))
+        grp = ctx.enter_context(tc.tile_pool(name="grp", bufs=6))
         keep = ctx.enter_context(tc.tile_pool(name="keep", bufs=1))
-        stage = ctx.enter_context(tc.tile_pool(name="stage", bufs=16))
         psum = ctx.enter_context(tc.psum_pool(name="psum", bufs=8))
 
         def load(src, c, col0, width, name):
-            t = raw.tile([P, PACK, width], BF16, name=name)
+            if width == 1024:
+                t = slots.tile([P, PACK, width], BF16, name=name, tag="slot")
+            else:
+                t = raw.tile([P, PACK, width], BF16, name=name)
             nc.sync.dma_start(
                 out=t[:],
                 in_=src[c * K_PASS : (c + 1) * K_PASS, col0 : col0 + width].rearrange(
@@ -76,34 +85,33 @@ def tile_ant_linear_kernel(tc, x, weight, bias, grid, grad_out, out):
                 x_codes[(n, c)] = keep.tile([P, N_TILE], U32, name="xc%d_%d" % (n, c), align_bytes=64)
                 x_scales[(n, c)] = keep.tile([P, N_TILE], U8, name="xs%d_%d" % (n, c), align_bytes=64)
 
-        pending = []
+        def operand(kind, a, c):
+            if kind == "g":
+                cols = slice(a * N_TILE, (a + 1) * N_TILE)
+                return g_raw[c], a * N_TILE, g_codes[c][:, cols], g_scales[c][:, cols], E5M2X4
+            t, col0 = x_raw[(a, c)]
+            return t, col0, x_codes[(a, c)][:], x_scales[(a, c)][:], E4M3X4
 
-        def flush(keep_last):
-            while len(pending) > keep_last:
-                grouped, codes, scales, fmt = pending.pop(0)
-                nc.vector.quantize_mx(
-                    out=codes.bitcast(fmt),
-                    scales=scales,
-                    in_=grouped[:].rearrange("p w j -> p (w j)"),
-                )
+        grouped_of = {}
 
-        def unit(src_tile, col0, codes, scales, fmt):
+        def regroup(key, on_scalar=False):
+            src_tile, col0 = operand(*key)[:2]
             grouped = grp.tile([P, N_TILE, PACK], BF16, name="grouped", align_bytes=64)
-            nc.vector.tensor_copy(
-                out=grouped[:].rearrange("p (c i) t -> p c t i", i=4),
-                in_=src_tile[:, :, col0 : col0 + N_TILE].rearrange("p t (c i) -> p c t i", i=4),
+            dst = grouped[:].rearrange("p (c i) t -> p c t i", i=4)
+            src = src_tile[:, :, col0 : col0 + N_TILE].rearrange("p t (c i) -> p c t i", i=4)
+            if on_scalar:
+                nc.scalar.copy(out=dst, in_=src)
+            else:
+                nc.vector.tensor_copy(out=dst, in_=src)
+            grouped_of[key] = grouped
+
+        def quantise(key):
+            codes, scales, fmt = operand(*key)[2:]
+            nc.vector.quantize_mx(
+                out=codes.bitcast(fmt),
+                scales=scales,
+                in_=grouped_of[key][:].rearrange("p w j -> p (w j)"),
             )
-            pending.append((grouped, codes, scales, fmt))
-            flush(1)
-
-        def quantise_g(c):
-            for h in range(OUT_ROWS // N_TILE):
-                cols = slice(h * N_TILE, (h + 1) * N_TILE)
-                unit(g_raw[c], h * N_TILE, g_codes[c][:, cols], g_scales[c][:, cols], E5M2X4)
-
-        def quantise_x(n, c):
-            t, col0 = x_raw[(n, c)]
-            unit(t, col0, x_codes[(n, c)][:], x_scales[(n, c)][:], E4M3X4)
 
         def mx(acc, n, m, c):
             rows = slice(m * M_TILE, (m + 1) * M_TILE)
@@ -117,47 +125,79 @@ def tile_ant_linear_kernel(tc, x, weight, bias, grid, grad_out, out):
                 stop=(c == PASSES - 1),
             )
 
+        group_of = {}
+        for first, count, tail in STORE_GROUPS:
+            for n in range(first, first + count):
+                group_of[n] = (first, count)
         stages = {}
 
         def leave(acc, n, m):
-            group, part = divmod(n, STORE_TILES)
-            if part == 0:
-                stages[m] = stage.tile([P, STORE_TILES * N_TILE], F32, name="res")
-            res = stages[m]
-            dst = res[:, part * N_TILE : (part + 1) * N_TILE]
-            if m in VECTOR_EVAC:
+            first, count = group_of[n]
+            if (first, m) not in stages:
+                stages[(first, m)] = slots.tile([P, count * N_TILE], F32, name="res", tag="slot")
+            res = stages[(first, m)]
+            dst = res[:, (n - first) * N_TILE : (n - first + 1) * N_TILE]
+            if vector_empties(n, m):
                 nc.vector.tensor_copy(out=dst, in_=acc[:])
             else:
                 nc.scalar.copy(out=dst, in_=acc[:])
-            if part == STORE_TILES - 1:
-                col0 = group * STORE_TILES * N_TILE
+            if n == first + count - 1:
                 nc.sync.dma_start(
-                    out=out[m * M_TILE : (m + 1) * M_TILE, col0 : col0 + STORE_TILES * N_TILE],
+                    out=out[m * M_TILE : (m + 1) * M_TILE, first * N_TILE : (first + count) * N_TILE],
                     in_=res[:],
                 )
 
-        quantise_g(0)
-        quantise_x(0, 0)
-        quantise_g(1)
-        quantise_x(0, 1)
-        quantise_x(1, 0)
-        quantise_x(1, 1)
-        flush(0)
+        def bank(n, m):
+            acc = psum.tile([P, N_TILE], F32, name="acc")
+            mx(acc, n, m, 0)
+            mx(acc, n, m, 1)
+            leave(acc, n, m)
 
+        regroup(("g", 0, 0))
+        regroup(("g", 1, 0), on_scalar=True)
+        quantise(("g", 0, 0))
+        quantise(("g", 1, 0))
+        regroup(("x", 0, 0))
+        regroup(("x", 1, 0), on_scalar=True)
+        quantise(("x", 0, 0))
         accs = [psum.tile([P, N_TILE], F32, name="acc") for m in range(M_TILES)]
         for m in range(M_TILES):
             mx(accs[m], 0, m, 0)
+        quantise(("x", 1, 0))
+        regroup(("g", 1, 1))
+        regroup(("g", 0, 1), on_scalar=True)
+        quantise(("g", 1, 1))
+        quantise(("g", 0, 1))
+        regroup(("x", 0, 1))
+        regroup(("x", 1, 1), on_scalar=True)
+        quantise(("x", 0, 1))
+        quantise(("x", 1, 1))
+
+        def prepare(n):
+            regroup(("x", n, 0))
+            regroup(("x", n, 1))
+            quantise(("x", n, 0))
+            quantise(("x", n, 1))
+
+        prepare(2)
         for m in range(M_TILES):
             mx(accs[m], 0, m, 1)
             leave(accs[m], 0, m)
 
-        for n in range(1, N_TILES):
-            if n + 1 < N_TILES:
-                quantise_x(n + 1, 0)
-                quantise_x(n + 1, 1)
-                flush(0)
-            for m in range(M_TILES):
-                acc = psum.tile([P, N_TILE], F32, name="acc")
-                mx(acc, n, m, 0)
-                mx(acc, n, m, 1)
-                leave(acc, n, m)
+        ready = 2
+        for first, count, tail in STORE_GROUPS:
+            for n in range(first, first + count - tail):
+                if n == 0:
+                    continue
+                while ready < min(n + 2 if n + 2 >= first + count - tail else n + 1, N_TILES - 1):
+                    ready += 1
+                    prepare(ready)
+                for m in range(M_TILES):
+                    bank(n, m)
+            if tail:
+                while ready < first + count - 1:
+                    ready += 1
+                    prepare(ready)
+                for m in range(M_TILES):
+                    for n in range(first + count - tail, first + count):
+                        bank(n, m)

@@ -24,12 +24,12 @@ N_TILES = OUT_COLS // N_TILE
 FLOPS = 2 * TOKENS * OUT_ROWS * OUT_COLS
 
 X_CHUNKS = (1024, 1024, 2048)
-STORE_GROUPS = ((0, 3, 0), (3, 3, 0), (6, 2, 0))
+STORE_GROUPS = ((0, 2, 0), (2, 2, 0), (4, 4, 3))
 PINNED = False
 
 
 def vector_empties(n, m):
-    return n >= 6 and m % 2 == 1
+    return (n == 0 and m % 2 == 1) or n == 6
 
 
 def tile_ant_linear_kernel(tc, x, weight, bias, grid, grad_out, out):
@@ -40,10 +40,11 @@ def tile_ant_linear_kernel(tc, x, weight, bias, grid, grad_out, out):
     with ExitStack() as ctx:
         if PINNED:
             ctx.enter_context(tc.manual_schedule())
-        slots = ctx.enter_context(tc.tile_pool(name="slots", bufs=15))
+        slots = ctx.enter_context(tc.tile_pool(name="slots", bufs=8))
         raw = ctx.enter_context(tc.tile_pool(name="raw", bufs=1))
         grp = ctx.enter_context(tc.tile_pool(name="grp", bufs=6))
         keep = ctx.enter_context(tc.tile_pool(name="keep", bufs=1))
+        stage = ctx.enter_context(tc.tile_pool(name="stage", bufs=14))
         psum = ctx.enter_context(tc.psum_pool(name="psum", bufs=8))
 
         def load(src, c, col0, width, name):
@@ -134,7 +135,10 @@ def tile_ant_linear_kernel(tc, x, weight, bias, grid, grad_out, out):
         def leave(acc, n, m):
             first, count = group_of[n]
             if (first, m) not in stages:
-                stages[(first, m)] = slots.tile([P, count * N_TILE], F32, name="res", tag="slot")
+                if count == 4:
+                    stages[(first, m)] = slots.tile([P, count * N_TILE], F32, name="wide", tag="slot")
+                else:
+                    stages[(first, m)] = stage.tile([P, count * N_TILE], F32, name="res")
             res = stages[(first, m)]
             dst = res[:, (n - first) * N_TILE : (n - first + 1) * N_TILE]
             if vector_empties(n, m):

from contextlib import ExitStack

import concourse.mybir as mybir

F32 = mybir.dt.float32
BF16 = mybir.dt.bfloat16
U32 = mybir.dt.uint32
U8 = mybir.dt.uint8
E4M3X4 = mybir.dt.float8_e4m3fn_x4
E5M2X4 = mybir.dt.float8_e5m2_x4

P = 128
PACK = 4
K_PASS = P * PACK
TOKENS = 1024
PASSES = TOKENS // K_PASS
OUT_ROWS = 1024
OUT_COLS = 4096
M_TILE = 128
N_TILE = 512
M_TILES = OUT_ROWS // M_TILE
N_TILES = OUT_COLS // N_TILE

FLOPS = 2 * TOKENS * OUT_ROWS * OUT_COLS

X_CHUNKS = (1024, 1024, 2048)
STORE_GROUPS = ((0, 2, 0), (2, 2, 0), (4, 4, 3))
PINNED = False


def vector_empties(n, m):
    return (n == 0 and m % 2 == 1) or n == 6


def tile_ant_linear_kernel(tc, x, weight, bias, grid, grad_out, out):
    nc = tc.nc
    x2 = x.flatten_outer_dims()
    g2 = grad_out.flatten_outer_dims()

    with ExitStack() as ctx:
        if PINNED:
            ctx.enter_context(tc.manual_schedule())
        slots = ctx.enter_context(tc.tile_pool(name="slots", bufs=8))
        raw = ctx.enter_context(tc.tile_pool(name="raw", bufs=1))
        grp = ctx.enter_context(tc.tile_pool(name="grp", bufs=6))
        keep = ctx.enter_context(tc.tile_pool(name="keep", bufs=1))
        stage = ctx.enter_context(tc.tile_pool(name="stage", bufs=14))
        psum = ctx.enter_context(tc.psum_pool(name="psum", bufs=8))

        def load(src, c, col0, width, name):
            if width == 1024:
                t = slots.tile([P, PACK, width], BF16, name=name, tag="slot")
            else:
                t = raw.tile([P, PACK, width], BF16, name=name)
            nc.sync.dma_start(
                out=t[:],
                in_=src[c * K_PASS : (c + 1) * K_PASS, col0 : col0 + width].rearrange(
                    "(p j) w -> p j w", j=PACK
                ),
            )
            return t

        g_raw = [None, None]
        x_raw = {}
        starts = [sum(X_CHUNKS[:i]) for i in range(len(X_CHUNKS))]

        def load_x(i, c):
            t = load(x2, c, starts[i], X_CHUNKS[i], "xr%d_%d" % (i, c))
            for n in range(starts[i] // N_TILE, (starts[i] + X_CHUNKS[i]) // N_TILE):
                x_raw[(n, c)] = (t, n * N_TILE - starts[i])

        g_raw[0] = load(g2, 0, 0, OUT_ROWS, "gr0")
        load_x(0, 0)
        g_raw[1] = load(g2, 1, 0, OUT_ROWS, "gr1")
        load_x(0, 1)
        for i in range(1, len(X_CHUNKS)):
            for c in range(PASSES):
                load_x(i, c)

        g_codes = [keep.tile([P, OUT_ROWS], U32, name="gc%d" % c, align_bytes=64) for c in range(PASSES)]
        g_scales = [keep.tile([P, OUT_ROWS], U8, name="gs%d" % c, align_bytes=64) for c in range(PASSES)]
        x_codes = {}
        x_scales = {}
        for n in range(N_TILES):
            for c in range(PASSES):
                x_codes[(n, c)] = keep.tile([P, N_TILE], U32, name="xc%d_%d" % (n, c), align_bytes=64)
                x_scales[(n, c)] = keep.tile([P, N_TILE], U8, name="xs%d_%d" % (n, c), align_bytes=64)

        def operand(kind, a, c):
            if kind == "g":
                cols = slice(a * N_TILE, (a + 1) * N_TILE)
                return g_raw[c], a * N_TILE, g_codes[c][:, cols], g_scales[c][:, cols], E5M2X4
            t, col0 = x_raw[(a, c)]
            return t, col0, x_codes[(a, c)][:], x_scales[(a, c)][:], E4M3X4

        grouped_of = {}

        def regroup(key, on_scalar=False):
            src_tile, col0 = operand(*key)[:2]
            grouped = grp.tile([P, N_TILE, PACK], BF16, name="grouped", align_bytes=64)
            dst = grouped[:].rearrange("p (c i) t -> p c t i", i=4)
            src = src_tile[:, :, col0 : col0 + N_TILE].rearrange("p t (c i) -> p c t i", i=4)
            if on_scalar:
                nc.scalar.copy(out=dst, in_=src)
            else:
                nc.vector.tensor_copy(out=dst, in_=src)
            grouped_of[key] = grouped

        def quantise(key):
            codes, scales, fmt = operand(*key)[2:]
            nc.vector.quantize_mx(
                out=codes.bitcast(fmt),
                scales=scales,
                in_=grouped_of[key][:].rearrange("p w j -> p (w j)"),
            )

        def mx(acc, n, m, c):
            rows = slice(m * M_TILE, (m + 1) * M_TILE)
            nc.tensor.matmul_mx(
                out=acc[:],
                lhsT=g_codes[c][:, rows].bitcast(E5M2X4),
                lhsT_scale=g_scales[c][:, rows],
                rhs=x_codes[(n, c)][:].bitcast(E4M3X4),
                rhs_scale=x_scales[(n, c)][:],
                start=(c == 0),
                stop=(c == PASSES - 1),
            )

        group_of = {}
        for first, count, tail in STORE_GROUPS:
            for n in range(first, first + count):
                group_of[n] = (first, count)
        stages = {}

        def leave(acc, n, m):
            first, count = group_of[n]
            if (first, m) not in stages:
                if count == 4:
                    stages[(first, m)] = slots.tile([P, count * N_TILE], F32, name="wide", tag="slot")
                else:
                    stages[(first, m)] = stage.tile([P, count * N_TILE], F32, name="res")
            res = stages[(first, m)]
            dst = res[:, (n - first) * N_TILE : (n - first + 1) * N_TILE]
            if vector_empties(n, m):
                nc.vector.tensor_copy(out=dst, in_=acc[:])
            else:
                nc.scalar.copy(out=dst, in_=acc[:])
            if n == first + count - 1:
                nc.sync.dma_start(
                    out=out[m * M_TILE : (m + 1) * M_TILE, first * N_TILE : (first + count) * N_TILE],
                    in_=res[:],
                )

        def bank(n, m):
            acc = psum.tile([P, N_TILE], F32, name="acc")
            mx(acc, n, m, 0)
            mx(acc, n, m, 1)
            leave(acc, n, m)

        regroup(("g", 0, 0))
        regroup(("g", 1, 0), on_scalar=True)
        quantise(("g", 0, 0))
        quantise(("g", 1, 0))
        regroup(("x", 0, 0))
        regroup(("x", 1, 0), on_scalar=True)
        quantise(("x", 0, 0))
        accs = [psum.tile([P, N_TILE], F32, name="acc") for m in range(M_TILES)]
        for m in range(M_TILES):
            mx(accs[m], 0, m, 0)
        quantise(("x", 1, 0))
        regroup(("g", 1, 1))
        regroup(("g", 0, 1), on_scalar=True)
        quantise(("g", 1, 1))
        quantise(("g", 0, 1))
        regroup(("x", 0, 1))
        regroup(("x", 1, 1), on_scalar=True)
        quantise(("x", 0, 1))
        quantise(("x", 1, 1))

        def prepare(n):
            regroup(("x", n, 0))
            regroup(("x", n, 1))
            quantise(("x", n, 0))
            quantise(("x", n, 1))

        prepare(2)
        for m in range(M_TILES):
            mx(accs[m], 0, m, 1)
            leave(accs[m], 0, m)

        ready = 2
        for first, count, tail in STORE_GROUPS:
            for n in range(first, first + count - tail):
                if n == 0:
                    continue
                while ready < min(n + 2 if n + 2 >= first + count - tail else n + 1, N_TILES - 1):
                    ready += 1
                    prepare(ready)
                for m in range(M_TILES):
                    bank(n, m)
            if tail:
                while ready < first + count - 1:
                    ready += 1
                    prepare(ready)
                for m in range(M_TILES):
                    for n in range(first + count - tail, first + count):
                        bank(n, m)
